import numpy as np
import ml_dtypes


def mxq(x, axis, fmt="e4m3"):
    dtype, down = {"e4m3": (ml_dtypes.float8_e4m3fn, 7), "e5m2": (ml_dtypes.float8_e5m2, 14)}[fmt]
    v = np.moveaxis(np.asarray(x, np.float32).astype(ml_dtypes.bfloat16).astype(np.float64), axis, -1)
    blocks = v.reshape(v.shape[:-1] + (-1, 32))
    amax = np.abs(blocks).max(-1, keepdims=True)
    byte = np.maximum(np.where(amax > 0, np.frexp(amax)[1] - 1 + 127, 0) - down, 1)
    scale = np.exp2(byte - 127.0)
    codes = (blocks / scale).astype(np.float32).astype(dtype).astype(np.float64)
    return np.moveaxis((codes * scale).reshape(v.shape), -1, axis)


WIDE = False


def mx_kscale(k):
    if not WIDE:
        return np.ones(k)
    levels = np.array([10, -10, 5, -5, 0])
    a = np.random.permutation(np.resize(levels, k // 512 * 4)).reshape(k // 512, 4)
    idx = np.arange(k)
    return np.exp2(a[idx // 512, idx % 128 // 32])


BF16 = ml_dtypes.bfloat16


def bf(x):
    return np.asarray(x, np.float32).astype(BF16)


def f64(x):
    return np.asarray(x).astype(np.float64)


KERNEL_SIZE = 4
B, T, D, H = 2, 256, 1024, 1024


def silu(v):
    return v / (1.0 + np.exp(-v))


def setup_inputs():
    W = KERNEL_SIZE
    s = mx_kscale(D)
    r = np.repeat(s, W)
    return {"x": bf(np.random.standard_normal((B, T, D)) * s),
            "w1": bf(np.random.standard_normal((H, D)) * 0.03 / s[None, :]),
            "w2_w": bf(np.random.standard_normal((D * W, H)) * 0.04 / r[:, None]),
            "w2_b": bf(np.random.standard_normal(D * W) * 0.2 / r)}


def reference(x, w1, w2_w, w2_b):
    x = f64(x)
    Bn, Tn, Dn = x.shape
    W = KERNEL_SIZE
    h = silu(mxq(x, 2, "e4m3") @ mxq(f64(w1), 1, "e4m3").T)
    flat_kernels = (mxq(h, 2, "e4m3") @ mxq(f64(w2_w), 1, "e4m3").T) + f64(w2_b)
    kernels = flat_kernels.reshape(Bn, Tn, Dn, W)
    x_pad = np.pad(x, ((0, 0), (W - 1, 0), (0, 0)))
    windows = np.stack([x_pad[:, w:w + Tn, :] for w in range(W)], axis=-1)
    out = np.sum(windows * kernels, axis=-1)
    return silu(out)

@@ -1,0 +1,295 @@
+from contextlib import ExitStack
+
+import concourse.bass as bass
+import concourse.mybir as mybir
+import concourse.tile as tile
+from concourse.masks import make_identity
+
+F32 = mybir.dt.float32
+BF16 = mybir.dt.bfloat16
+U32 = mybir.dt.uint32
+U8 = mybir.dt.uint8
+FP8X4 = mybir.dt.float8_e4m3fn_x4
+ACT = mybir.ActivationFunctionType
+ALU = mybir.AluOpType
+
+P = 128
+TOK = 512
+D = 1024
+H = 1024
+W = 4
+PAD = 8
+TB = 256 + PAD
+
+FLOPS = 2 * TOK * D * H + 2 * TOK * H * D * W
+
+
+def tile_dynamicshortconvolution_kernel(tc, x, w1, w2_w, w2_b, out):
+    nc = tc.nc
+    xf = x.flatten_outer_dims()
+    of = out.flatten_outer_dims()
+
+    with ExitStack() as ctx:
+        const = ctx.enter_context(tc.tile_pool(name="const", bufs=1))
+        raw = ctx.enter_context(tc.tile_pool(name="raw", bufs=1))
+        keep = ctx.enter_context(tc.tile_pool(name="keep", bufs=1))
+        w1gp = ctx.enter_context(tc.tile_pool(name="w1gp", bufs=3))
+        w2gp = ctx.enter_context(tc.tile_pool(name="w2gp", bufs=2))
+        w2cp = ctx.enter_context(tc.tile_pool(name="w2cp", bufs=4))
+        prodp = ctx.enter_context(tc.tile_pool(name="prodp", bufs=2))
+        sump = ctx.enter_context(tc.tile_pool(name="sump", bufs=4))
+        outp = ctx.enter_context(tc.tile_pool(name="outp", bufs=4))
+        ps_t = ctx.enter_context(tc.psum_pool(name="ps_t", bufs=3))
+        ps_k = ctx.enter_context(tc.psum_pool(name="ps_k", bufs=4))
+        ps_o = ctx.enter_context(tc.psum_pool(name="ps_o", bufs=1))
+        ctx.enter_context(tc.manual_schedule())
+
+        bias_bf = const.tile([P, 32], BF16, name="bias_bf")
+        nc.scalar.dma_start(
+            out=bias_bf[:].rearrange("p (u j) -> p u j", u=4),
+            in_=w2_b.rearrange("(u p j) -> p u j", u=4, p=P, j=8),
+        )
+        warm = const.tile([P, 2], F32, name="warm")
+        nc.vector.memset(warm[:], 0.0)
+        nc.scalar.activation(out=warm[:, 1:2], in_=warm[:, 0:1], func=ACT.Silu)
+        ident = const.tile([P, P], F32, name="ident")
+        make_identity(nc, ident[:])
+
+        xg = [keep.tile([P, 2 * TB * 4], BF16, name="xg%d" % g, align_bytes=64) for g in range(2)]
+        xgw = [t[:].bitcast(F32).rearrange("p (b t u) -> p b t u", b=2, t=TB, u=2) for t in xg]
+        xgq = [t[:].rearrange("p (b t q) -> p b t q", b=2, t=TB, q=4) for t in xg]
+        for g in range(2):
+            for b in range(2):
+                nc.gpsimd.memset(xgw[g][:, b, 0:PAD, :], 0.0)
+
+        x_sb = []
+        for b in range(2):
+            t = raw.tile([P, 2 * D], BF16, name="x_sb%d" % b)
+            nc.sync.dma_start(
+                out=t[:].rearrange("p (c d) -> p c d", c=2),
+                in_=xf[256 * b : 256 * b + 256, :].rearrange("(c p) d -> p c d", p=P),
+            )
+            x_sb.append(t[:].bitcast(F32))
+        w1_sb = []
+        for a in range(4):
+            t = raw.tile([P, 2 * D], BF16, name="w1_sb%d" % a)
+            nc.sync.dma_start(
+                out=t[:].rearrange("p (e d) -> p e d", e=2),
+                in_=w1[256 * a : 256 * a + 256, :].rearrange("(p e) d -> p e d", e=2),
+            )
+            w1_sb.append(t[:].bitcast(F32))
+        w2_sb = []
+        for i in range(8):
+            u, e = divmod(i, 2)
+            t = raw.tile([P, 4 * H], BF16, name="w2_sb%d" % i)
+            nc.sync.dma_start(
+                out=t[:].rearrange("p (j h) -> p j h", j=4),
+                in_=w2_w[1024 * u : 1024 * u + 1024, :].rearrange("(p j) h -> p j h", j=8)[:, 4 * e : 4 * e + 4, :],
+            )
+            w2_sb.append(t[:].bitcast(F32))
+
+        bias = const.tile([P, 32], F32, name="bias")
+        nc.vector.tensor_copy(out=bias[:], in_=bias_bf[:])
+
+        xc = keep.tile([P, 2 * TOK], U32, name="xc", align_bytes=64)
+        xs = keep.tile([P, 2 * TOK], U8, name="xs", align_bytes=64)
+        w1c = keep.tile([P, 4 * 512], U32, name="w1c", align_bytes=64)
+        w1s = keep.tile([P, 4 * 512], U8, name="w1s", align_bytes=64)
+        hg = [keep.tile([P, TOK * 4], BF16, name="hg%d" % g, align_bytes=64) for g in range(2)]
+        hc = keep.tile([P, 2 * TOK], U32, name="hc", align_bytes=64)
+        hs = keep.tile([P, 2 * TOK], U8, name="hs", align_bytes=64)
+
+        def transposes(src, offsets):
+            tp = ps_t.tile([P, 512], F32, name="tp", tag="tp")
+            for k, off in enumerate(offsets):
+                nc.tensor.transpose(tp[:, 128 * k : 128 * k + 128], src[:, off : off + 128], ident[:])
+            return tp
+
+        def regroup(eng_copy, dst_words, tp):
+            eng_copy(
+                out=dst_words.rearrange("p (c u) -> p c u", u=2),
+                in_=tp[:].rearrange("p (u c) -> p c u", u=2),
+            )
+
+        def quant(src, codes, scales, lo, n):
+            nc.vector.quantize_mx(
+                out=codes[:, lo : lo + n].bitcast(FP8X4), scales=scales[:, lo : lo + n], in_=src
+            )
+
+        vcopy = nc.vector.tensor_copy
+        scopy = nc.scalar.copy
+
+        def tx(g, b):
+            return transposes(x_sb[b], [cc * 512 + 256 * g + 128 * u for u in range(2) for cc in range(2)])
+
+        def cx(g, b, tp):
+            vcopy(out=xgw[g][:, b, PAD:TB, :], in_=tp[:].rearrange("p (u c) -> p c u", u=2))
+
+        def qx(g, b):
+            lo = (b * TB + PAD) * 4
+            quant(xg[g][:, lo : lo + 1024], xc, xs, g * 512 + 256 * b, 256)
+
+        cx(0, 0, tx(0, 0))
+        cx(1, 0, tx(1, 0))
+        cx(0, 1, tx(0, 1))
+        qx(0, 0)
+        cx(1, 1, tx(1, 1))
+        qx(1, 0)
+        qx(0, 1)
+        qx(1, 1)
+
+        w1g = []
+        for a in range(4):
+            gt = w1gp.tile([P, 2048], BF16, name="w1g", tag="w1g", align_bytes=64)
+            w1g.append(gt)
+            gw = gt[:].bitcast(F32)
+            for g in range(2):
+                tp = transposes(w1_sb[a], [e * 512 + 256 * g + 128 * u for u in range(2) for e in range(2)])
+                regroup(scopy if g == 0 else vcopy, gw[:, g * 512 : g * 512 + 512], tp)
+            if a > 0:
+                quant(w1g[a - 1][:], w1c, w1s, (a - 1) * 512, 512)
+        quant(w1g[3][:], w1c, w1s, 3 * 512, 512)
+
+        w2g = {}
+        w2c = {}
+        w2s = {}
+
+        def tw2(i):
+            gt = w2gp.tile([P, 4096], BF16, name="w2g", tag="w2g", align_bytes=64)
+            w2g[i] = gt
+            gw = gt[:].bitcast(F32)
+            for q in range(4):
+                gg, wp = divmod(q, 2)
+                tp = transposes(
+                    w2_sb[i], [(2 * wp + ww) * 512 + 256 * gg + 128 * u for u in range(2) for ww in range(2)]
+                )
+                regroup(scopy, gw[:, q * 512 : q * 512 + 512], tp)
+
+        def qw2(i):
+            w2c[i] = w2cp.tile([P, 1024], U32, name="w2c", tag="w2c", align_bytes=64)
+            w2s[i] = w2cp.tile([P, 1024], U8, name="w2s", tag="w2s", align_bytes=64)
+            quant(w2g[i][:], w2c[i], w2s[i], 0, 1024)
+
+        def mm1(gg, c):
+            kk = ps_k.tile([P, 512], F32, name="kk", tag="kk")
+            for t in range(4):
+                a = 2 * gg + t // 2
+                e = t % 2
+                for g in range(2):
+                    lo = a * 512 + g * 256 + e * 128
+                    ro = g * 512 + 128 * c
+                    nc.tensor.matmul_mx(
+                        out=kk[:, 128 * t : 128 * t + 128],
+                        lhsT=w1c[:, lo : lo + 128].bitcast(FP8X4),
+                        lhsT_scale=w1s[:, lo : lo + 128],
+                        rhs=xc[:, ro : ro + 128].bitcast(FP8X4),
+                        rhs_scale=xs[:, ro : ro + 128],
+                        start=(g == 0),
+                        stop=(g == 1),
+                    )
+            nc.scalar.activation(
+                out=hg[gg][:, c * 512 : c * 512 + 512].rearrange("p (r t) -> p r t", t=4),
+                in_=kk[:].rearrange("p (t r) -> p r t", t=4),
+                func=ACT.Silu,
+            )
+
+        def qh(gg, half):
+            quant(hg[gg][:, half * 1024 : half * 1024 + 1024], hc, hs, gg * 512 + half * 256, 256)
+
+        prod = {}
+        sums = {}
+
+        def mx(i, w):
+            u, e = divmod(i, 2)
+            if w == 0:
+                prod[i] = prodp.tile([P, 4 * TOK], F32, name="prod", tag="prod")
+            kk = ps_k.tile([P, 512], F32, name="kk", tag="kk")
+            for gg in range(2):
+                lo = gg * 512 + w * 128
+                nc.tensor.matmul_mx(
+                    out=kk[:],
+                    lhsT=w2c[i][:, lo : lo + 128].bitcast(FP8X4),
+                    lhsT_scale=w2s[i][:, lo : lo + 128],
+                    rhs=hc[:, gg * 512 : gg * 512 + 512].bitcast(FP8X4),
+                    rhs_scale=hs[:, gg * 512 : gg * 512 + 512],
+                    start=(gg == 0),
+                    stop=(gg == 1),
+                )
+            col = u * 8 + 4 * e + w
+            nc.vector.scalar_tensor_tensor(
+                out=prod[i][:, w * 512 : w * 512 + 512].rearrange("p (b t) -> p b t", b=2),
+                in0=kk[:].rearrange("p (b t) -> p b t", b=2),
+                scalar=bias[:, col : col + 1],
+                in1=xgq[u // 2][:, :, PAD - 3 + w : PAD - 3 + w + 256, 2 * (u % 2) + e],
+                op0=ALU.add,
+                op1=ALU.mult,
+            )
+
+        def add(i):
+            sums[i] = sump.tile([P, 2 * TOK], F32, name="sums", tag="sums")
+            nc.gpsimd.tensor_tensor(
+                out=sums[i][:], in0=prod[i][:, 0:1024], in1=prod[i][:, 1024:2048], op=ALU.add
+            )
+
+        def bt(u, cp, pool, tag):
+            ob = pool.tile([P, 512], F32, name=tag, tag=tag)
+            for cc in range(2):
+                c = 2 * cp + cc
+                for e in range(2):
+                    i = 2 * u + e
+                    if i in sums:
+                        terms = [sums[i][:, k * 512 + 128 * c : k * 512 + 128 * c + 128] for k in range(2)]
+                    else:
+                        terms = [prod[i][:, k * 512 + 128 * c : k * 512 + 128 * c + 128] for k in range(4)]
+                    lo = cc * 256 + e * 128
+                    for k, term in enumerate(terms):
+                        nc.tensor.matmul(
+                            out=ob[:, lo : lo + 128],
+                            lhsT=term,
+                            rhs=ident[:],
+                            is_transpose=True,
+                            start=(k == 0),
+                            stop=(k == len(terms) - 1),
+                        )
+            ot = outp.tile([P, 512], F32, name="ot", tag="ot")
+            nc.scalar.activation(
+                out=ot[:].rearrange("t (c p e) -> t c p e", c=2, e=2),
+                in_=ob[:].rearrange("t (c e p) -> t c p e", c=2, e=2),
+                func=ACT.Silu,
+            )
+            nc.sync.dma_start(
+                out=of[256 * cp : 256 * cp + 256, 256 * u : 256 * u + 256].rearrange("(c p) d -> p c d", p=P),
+                in_=ot[:].rearrange("p (c d) -> p c d", c=2),
+            )
+
+        for c in range(4):
+            mm1(0, c)
+        tw2(0)
+        qh(0, 0)
+        qh(0, 1)
+        for c in range(4):
+            mm1(1, c)
+            if c == 1:
+                qw2(0)
+                qh(1, 0)
+        tw2(1)
+        qh(1, 1)
+        qw2(1)
+
+        back = {3: [(0, 0)], 4: [(0, 1)], 5: [(1, 0)], 6: [(1, 1)], 7: [(2, 0), (2, 1)]}
+        for i in range(8):
+            if i + 2 < 8:
+                tw2(i + 2)
+            for n, (u, cp) in enumerate(back.get(i, [])):
+                if n == 0:
+                    bt(u, cp, ps_o, "ob")
+                else:
+                    bt(u, cp, ps_t, "tp")
+            for w in range(4):
+                if w == 3 and i + 2 < 8:
+                    qw2(i + 2)
+                mx(i, w)
+            if i < 7:
+                add(i)
+        bt(3, 0, ps_o, "ob")
+        bt(3, 1, ps_t, "tp")

@@ -1,8 +1,6 @@
 from contextlib import ExitStack
 
-import concourse.bass as bass
 import concourse.mybir as mybir
-import concourse.tile as tile
 from concourse.masks import make_identity
 
 F32 = mybir.dt.float32
@@ -36,13 +34,17 @@ def tile_dynamicshortconvolution_kernel(tc, x, w1, w2_w, w2_b, out):
         w1gp = ctx.enter_context(tc.tile_pool(name="w1gp", bufs=3))
         w2gp = ctx.enter_context(tc.tile_pool(name="w2gp", bufs=2))
         w2cp = ctx.enter_context(tc.tile_pool(name="w2cp", bufs=4))
-        prodp = ctx.enter_context(tc.tile_pool(name="prodp", bufs=2))
+        prodp = ctx.enter_context(tc.tile_pool(name="prodp", bufs=3))
         sump = ctx.enter_context(tc.tile_pool(name="sump", bufs=4))
         outp = ctx.enter_context(tc.tile_pool(name="outp", bufs=4))
-        ps_t = ctx.enter_context(tc.psum_pool(name="ps_t", bufs=3))
-        ps_k = ctx.enter_context(tc.psum_pool(name="ps_k", bufs=4))
+        ps_t = ctx.enter_context(tc.psum_pool(name="ps_t", bufs=4))
+        ps_k = ctx.enter_context(tc.psum_pool(name="ps_k", bufs=3))
         ps_o = ctx.enter_context(tc.psum_pool(name="ps_o", bufs=1))
         ctx.enter_context(tc.manual_schedule())
+        banks = {"tp": ps_t, "kk": ps_k, "ob": ps_o}
+
+        def bank(tag):
+            return banks[tag].tile([P, 512], F32, name=tag, tag=tag)
 
         bias_bf = const.tile([P, 32], BF16, name="bias_bf")
         nc.scalar.dma_start(
@@ -55,20 +57,15 @@ def tile_dynamicshortconvolution_kernel(tc, x, w1, w2_w, w2_b, out):
         ident = const.tile([P, P], F32, name="ident")
         make_identity(nc, ident[:])
 
-        xg = [keep.tile([P, 2 * TB * 4], BF16, name="xg%d" % g, align_bytes=64) for g in range(2)]
-        xgw = [t[:].bitcast(F32).rearrange("p (b t u) -> p b t u", b=2, t=TB, u=2) for t in xg]
-        xgq = [t[:].rearrange("p (b t q) -> p b t q", b=2, t=TB, q=4) for t in xg]
-        for g in range(2):
-            for b in range(2):
-                nc.gpsimd.memset(xgw[g][:, b, 0:PAD, :], 0.0)
+        xg = keep.tile([P, 4 * TB * 4], BF16, name="xg", align_bytes=64)
+        xgw = xg[:].bitcast(F32).rearrange("p (g b t u) -> p g b t u", g=2, b=2, t=TB, u=2)
+        xgq = xg[:].rearrange("p (g b t q) -> p g b t q", g=2, b=2, t=TB, q=4)
+        nc.gpsimd.memset(xgw[:, :, :, 0:PAD, :], 0.0)
 
         x_sb = []
-        for b in range(2):
-            t = raw.tile([P, 2 * D], BF16, name="x_sb%d" % b)
-            nc.sync.dma_start(
-                out=t[:].rearrange("p (c d) -> p c d", c=2),
-                in_=xf[256 * b : 256 * b + 256, :].rearrange("(c p) d -> p c d", p=P),
-            )
+        for c in range(4):
+            t = raw.tile([P, D], BF16, name="x_sb%d" % c)
+            nc.sync.dma_start(out=t[:], in_=xf[128 * c : 128 * c + 128, :])
             x_sb.append(t[:].bitcast(F32))
         w1_sb = []
         for a in range(4):
@@ -99,8 +96,11 @@ def tile_dynamicshortconvolution_kernel(tc, x, w1, w2_w, w2_b, out):
         hc = keep.tile([P, 2 * TOK], U32, name="hc", align_bytes=64)
         hs = keep.tile([P, 2 * TOK], U8, name="hs", align_bytes=64)
 
+        vcopy = nc.vector.tensor_copy
+        scopy = nc.scalar.copy
+
         def transposes(src, offsets):
-            tp = ps_t.tile([P, 512], F32, name="tp", tag="tp")
+            tp = bank("tp")
             for k, off in enumerate(offsets):
                 nc.tensor.transpose(tp[:, 128 * k : 128 * k + 128], src[:, off : off + 128], ident[:])
             return tp
@@ -116,24 +116,24 @@ def tile_dynamicshortconvolution_kernel(tc, x, w1, w2_w, w2_b, out):
                 out=codes[:, lo : lo + n].bitcast(FP8X4), scales=scales[:, lo : lo + n], in_=src
             )
 
-        vcopy = nc.vector.tensor_copy
-        scopy = nc.scalar.copy
-
-        def tx(g, b):
-            return transposes(x_sb[b], [cc * 512 + 256 * g + 128 * u for u in range(2) for cc in range(2)])
-
-        def cx(g, b, tp):
-            vcopy(out=xgw[g][:, b, PAD:TB, :], in_=tp[:].rearrange("p (u c) -> p c u", u=2))
+        def tx(c, eng_copy):
+            tp = transposes(x_sb[c], [256 * g + 128 * u for g in range(2) for u in range(2)])
+            b, cc = divmod(c, 2)
+            lo = PAD + 128 * cc
+            eng_copy(
+                out=xgw[:, :, b, lo : lo + 128, :],
+                in_=tp[:].rearrange("p (g u t) -> p g t u", g=2, u=2),
+            )
 
         def qx(g, b):
-            lo = (b * TB + PAD) * 4
-            quant(xg[g][:, lo : lo + 1024], xc, xs, g * 512 + 256 * b, 256)
+            lo = ((g * 2 + b) * TB + PAD) * 4
+            quant(xg[:, lo : lo + 1024], xc, xs, g * 512 + 256 * b, 256)
 
-        cx(0, 0, tx(0, 0))
-        cx(1, 0, tx(1, 0))
-        cx(0, 1, tx(0, 1))
+        tx(0, vcopy)
+        tx(1, scopy)
+        tx(2, vcopy)
         qx(0, 0)
-        cx(1, 1, tx(1, 1))
+        tx(3, scopy)
         qx(1, 0)
         qx(0, 1)
         qx(1, 1)
@@ -154,16 +154,15 @@ def tile_dynamicshortconvolution_kernel(tc, x, w1, w2_w, w2_b, out):
         w2c = {}
         w2s = {}
 
-        def tw2(i):
-            gt = w2gp.tile([P, 4096], BF16, name="w2g", tag="w2g", align_bytes=64)
-            w2g[i] = gt
-            gw = gt[:].bitcast(F32)
-            for q in range(4):
-                gg, wp = divmod(q, 2)
-                tp = transposes(
-                    w2_sb[i], [(2 * wp + ww) * 512 + 256 * gg + 128 * u for u in range(2) for ww in range(2)]
-                )
-                regroup(scopy, gw[:, q * 512 : q * 512 + 512], tp)
+        def tw2q(i, q, eng_copy):
+            if q == 0:
+                w2g[i] = w2gp.tile([P, 4096], BF16, name="w2g", tag="w2g", align_bytes=64)
+            gw = w2g[i][:].bitcast(F32)
+            gg, wp = divmod(q, 2)
+            tp = transposes(
+                w2_sb[i], [(2 * wp + ww) * 512 + 256 * gg + 128 * u for u in range(2) for ww in range(2)]
+            )
+            regroup(eng_copy, gw[:, q * 512 : q * 512 + 512], tp)
 
         def qw2(i):
             w2c[i] = w2cp.tile([P, 1024], U32, name="w2c", tag="w2c", align_bytes=64)
@@ -171,7 +170,7 @@ def tile_dynamicshortconvolution_kernel(tc, x, w1, w2_w, w2_b, out):
             quant(w2g[i][:], w2c[i], w2s[i], 0, 1024)
 
         def mm1(gg, c):
-            kk = ps_k.tile([P, 512], F32, name="kk", tag="kk")
+            kk = bank("kk")
             for t in range(4):
                 a = 2 * gg + t // 2
                 e = t % 2
@@ -199,11 +198,11 @@ def tile_dynamicshortconvolution_kernel(tc, x, w1, w2_w, w2_b, out):
         prod = {}
         sums = {}
 
-        def mx(i, w):
+        def mx(i, w, tag):
             u, e = divmod(i, 2)
             if w == 0:
                 prod[i] = prodp.tile([P, 4 * TOK], F32, name="prod", tag="prod")
-            kk = ps_k.tile([P, 512], F32, name="kk", tag="kk")
+            kk = bank(tag)
             for gg in range(2):
                 lo = gg * 512 + w * 128
                 nc.tensor.matmul_mx(
@@ -220,7 +219,7 @@ def tile_dynamicshortconvolution_kernel(tc, x, w1, w2_w, w2_b, out):
                 out=prod[i][:, w * 512 : w * 512 + 512].rearrange("p (b t) -> p b t", b=2),
                 in0=kk[:].rearrange("p (b t) -> p b t", b=2),
                 scalar=bias[:, col : col + 1],
-                in1=xgq[u // 2][:, :, PAD - 3 + w : PAD - 3 + w + 256, 2 * (u % 2) + e],
+                in1=xgq[:, u // 2, :, PAD - 3 + w : PAD - 3 + w + 256, 2 * (u % 2) + e],
                 op0=ALU.add,
                 op1=ALU.mult,
             )
@@ -231,26 +230,23 @@ def tile_dynamicshortconvolution_kernel(tc, x, w1, w2_w, w2_b, out):
                 out=sums[i][:], in0=prod[i][:, 0:1024], in1=prod[i][:, 1024:2048], op=ALU.add
             )
 
-        def bt(u, cp, pool, tag):
-            ob = pool.tile([P, 512], F32, name=tag, tag=tag)
+        def bt_part(ob, u, cp, e):
+            i = 2 * u + e
+            src, n = (sums[i], 2) if i in sums else (prod[i], 4)
             for cc in range(2):
                 c = 2 * cp + cc
-                for e in range(2):
-                    i = 2 * u + e
-                    if i in sums:
-                        terms = [sums[i][:, k * 512 + 128 * c : k * 512 + 128 * c + 128] for k in range(2)]
-                    else:
-                        terms = [prod[i][:, k * 512 + 128 * c : k * 512 + 128 * c + 128] for k in range(4)]
-                    lo = cc * 256 + e * 128
-                    for k, term in enumerate(terms):
-                        nc.tensor.matmul(
-                            out=ob[:, lo : lo + 128],
-                            lhsT=term,
-                            rhs=ident[:],
-                            is_transpose=True,
-                            start=(k == 0),
-                            stop=(k == len(terms) - 1),
-                        )
+                lo = cc * 256 + e * 128
+                for k in range(n):
+                    nc.tensor.matmul(
+                        out=ob[:, lo : lo + 128],
+                        lhsT=src[:, k * 512 + 128 * c : k * 512 + 128 * c + 128],
+                        rhs=ident[:],
+                        is_transpose=True,
+                        start=(k == 0),
+                        stop=(k == n - 1),
+                    )
+
+        def bt_fin(ob, u, cp):
             ot = outp.tile([P, 512], F32, name="ot", tag="ot")
             nc.scalar.activation(
                 out=ot[:].rearrange("t (c p e) -> t c p e", c=2, e=2),
@@ -262,34 +258,48 @@ def tile_dynamicshortconvolution_kernel(tc, x, w1, w2_w, w2_b, out):
                 in_=ot[:].rearrange("p (c d) -> p c d", c=2),
             )
 
+        def bt(u, cp, tag):
+            ob = bank(tag)
+            bt_part(ob, u, cp, 0)
+            bt_part(ob, u, cp, 1)
+            bt_fin(ob, u, cp)
+
         for c in range(4):
             mm1(0, c)
-        tw2(0)
         qh(0, 0)
         qh(0, 1)
         for c in range(4):
             mm1(1, c)
             if c == 1:
-                qw2(0)
                 qh(1, 0)
-        tw2(1)
-        qh(1, 1)
-        qw2(1)
+        for i in range(2):
+            for q in range(4):
+                tw2q(i, q, vcopy if q % 2 else scopy)
+                if i == 0 and q == 1:
+                    qh(1, 1)
+            qw2(i)
 
-        back = {3: [(0, 0)], 4: [(0, 1)], 5: [(1, 0)], 6: [(1, 1)], 7: [(2, 0), (2, 1)]}
+        back = {3: (0, 0), 4: (0, 1), 5: (1, 0), 6: (1, 1)}
+        late = ["kk", "kk", "kk", "tp", "tp", "tp", "tp", "kk"]
         for i in range(8):
             if i + 2 < 8:
-                tw2(i + 2)
-            for n, (u, cp) in enumerate(back.get(i, [])):
-                if n == 0:
-                    bt(u, cp, ps_o, "ob")
-                else:
-                    bt(u, cp, ps_t, "tp")
+                for q in range(4):
+                    tw2q(i + 2, q, scopy)
+            if i in back:
+                bt(back[i][0], back[i][1], "ob")
             for w in range(4):
                 if w == 3 and i + 2 < 8:
                     qw2(i + 2)
-                mx(i, w)
+                mx(i, w, late[(i - 6) * 4 + w] if i >= 6 else "kk")
             if i < 7:
                 add(i)
-        bt(3, 0, ps_o, "ob")
-        bt(3, 1, ps_t, "tp")
+        bt(2, 0, "ob")
+        bt(2, 1, "kk")
+        ob0 = bank("kk")
+        ob1 = bank("tp")
+        bt_part(ob0, 3, 0, 0)
+        bt_part(ob1, 3, 1, 0)
+        bt_part(ob0, 3, 0, 1)
+        bt_fin(ob0, 3, 0)
+        bt_part(ob1, 3, 1, 1)
+        bt_fin(ob1, 3, 1)

@@ -37,14 +37,14 @@ def tile_dynamicshortconvolution_kernel(tc, x, w1, w2_w, w2_b, out):
         prodp = ctx.enter_context(tc.tile_pool(name="prodp", bufs=3))
         sump = ctx.enter_context(tc.tile_pool(name="sump", bufs=4))
         outp = ctx.enter_context(tc.tile_pool(name="outp", bufs=4))
-        ps_t = ctx.enter_context(tc.psum_pool(name="ps_t", bufs=4))
-        ps_k = ctx.enter_context(tc.psum_pool(name="ps_k", bufs=3))
-        ps_o = ctx.enter_context(tc.psum_pool(name="ps_o", bufs=1))
+        psum = ctx.enter_context(tc.psum_pool(name="psum", bufs=1))
         ctx.enter_context(tc.manual_schedule())
-        banks = {"tp": ps_t, "kk": ps_k, "ob": ps_o}
+        taken = []
 
-        def bank(tag):
-            return banks[tag].tile([P, 512], F32, name=tag, tag=tag)
+        def bank():
+            k = len(taken) % 8
+            taken.append(k)
+            return psum.tile([P, 512], F32, name="bank%d" % k, tag="bank%d" % k)
 
         bias_bf = const.tile([P, 32], BF16, name="bias_bf")
         nc.scalar.dma_start(
@@ -63,18 +63,27 @@ def tile_dynamicshortconvolution_kernel(tc, x, w1, w2_w, w2_b, out):
         nc.gpsimd.memset(xgw[:, :, :, 0:PAD, :], 0.0)
 
         x_sb = []
-        for c in range(4):
+        w1_sb = []
+
+        def load_x(c):
             t = raw.tile([P, D], BF16, name="x_sb%d" % c)
             nc.sync.dma_start(out=t[:], in_=xf[128 * c : 128 * c + 128, :])
             x_sb.append(t[:].bitcast(F32))
-        w1_sb = []
-        for a in range(4):
+
+        def load_w1(a):
             t = raw.tile([P, 2 * D], BF16, name="w1_sb%d" % a)
             nc.sync.dma_start(
                 out=t[:].rearrange("p (e d) -> p e d", e=2),
                 in_=w1[256 * a : 256 * a + 256, :].rearrange("(p e) d -> p e d", e=2),
             )
             w1_sb.append(t[:].bitcast(F32))
+
+        load_w1(0)
+        load_w1(1)
+        for c in range(4):
+            load_x(c)
+        load_w1(2)
+        load_w1(3)
         w2_sb = []
         for i in range(8):
             u, e = divmod(i, 2)
@@ -100,7 +109,7 @@ def tile_dynamicshortconvolution_kernel(tc, x, w1, w2_w, w2_b, out):
         scopy = nc.scalar.copy
 
         def transposes(src, offsets):
-            tp = bank("tp")
+            tp = bank()
             for k, off in enumerate(offsets):
                 nc.tensor.transpose(tp[:, 128 * k : 128 * k + 128], src[:, off : off + 128], ident[:])
             return tp
@@ -129,26 +138,17 @@ def tile_dynamicshortconvolution_kernel(tc, x, w1, w2_w, w2_b, out):
             lo = ((g * 2 + b) * TB + PAD) * 4
             quant(xg[:, lo : lo + 1024], xc, xs, g * 512 + 256 * b, 256)
 
-        tx(0, vcopy)
-        tx(1, scopy)
-        tx(2, vcopy)
-        qx(0, 0)
-        tx(3, scopy)
-        qx(1, 0)
-        qx(0, 1)
-        qx(1, 1)
+        w1g = {}
 
-        w1g = []
-        for a in range(4):
-            gt = w1gp.tile([P, 2048], BF16, name="w1g", tag="w1g", align_bytes=64)
-            w1g.append(gt)
-            gw = gt[:].bitcast(F32)
-            for g in range(2):
-                tp = transposes(w1_sb[a], [e * 512 + 256 * g + 128 * u for u in range(2) for e in range(2)])
-                regroup(scopy if g == 0 else vcopy, gw[:, g * 512 : g * 512 + 512], tp)
-            if a > 0:
-                quant(w1g[a - 1][:], w1c, w1s, (a - 1) * 512, 512)
-        quant(w1g[3][:], w1c, w1s, 3 * 512, 512)
+        def tw1(a, g, eng_copy):
+            if g == 0:
+                w1g[a] = w1gp.tile([P, 2048], BF16, name="w1g", tag="w1g", align_bytes=64)
+            gw = w1g[a][:].bitcast(F32)
+            tp = transposes(w1_sb[a], [e * 512 + 256 * g + 128 * u for u in range(2) for e in range(2)])
+            regroup(eng_copy, gw[:, g * 512 : g * 512 + 512], tp)
+
+        def qw1(a):
+            quant(w1g[a][:], w1c, w1s, a * 512, 512)
 
         w2g = {}
         w2c = {}
@@ -170,7 +170,7 @@ def tile_dynamicshortconvolution_kernel(tc, x, w1, w2_w, w2_b, out):
             quant(w2g[i][:], w2c[i], w2s[i], 0, 1024)
 
         def mm1(gg, c):
-            kk = bank("kk")
+            kk = bank()
             for t in range(4):
                 a = 2 * gg + t // 2
                 e = t % 2
@@ -198,11 +198,11 @@ def tile_dynamicshortconvolution_kernel(tc, x, w1, w2_w, w2_b, out):
         prod = {}
         sums = {}
 
-        def mx(i, w, tag):
+        def mx(i, w):
             u, e = divmod(i, 2)
             if w == 0:
                 prod[i] = prodp.tile([P, 4 * TOK], F32, name="prod", tag="prod")
-            kk = bank(tag)
+            kk = bank()
             for gg in range(2):
                 lo = gg * 512 + w * 128
                 nc.tensor.matmul_mx(
@@ -258,45 +258,69 @@ def tile_dynamicshortconvolution_kernel(tc, x, w1, w2_w, w2_b, out):
                 in_=ot[:].rearrange("p (c d) -> p c d", c=2),
             )
 
-        def bt(u, cp, tag):
-            ob = bank(tag)
+        def bt(u, cp):
+            ob = bank()
             bt_part(ob, u, cp, 0)
             bt_part(ob, u, cp, 1)
             bt_fin(ob, u, cp)
 
-        for c in range(4):
-            mm1(0, c)
+        tw1(0, 0, scopy)
+        tw1(0, 1, vcopy)
+        tw1(1, 0, scopy)
+        tw1(1, 1, vcopy)
+        qw1(0)
+        tx(0, scopy)
+        tx(1, scopy)
+        qw1(1)
+        tx(2, scopy)
+        qx(0, 0)
+        qx(1, 0)
+        tx(3, scopy)
+        tw1(2, 0, scopy)
+        tw1(2, 1, vcopy)
+        qx(0, 1)
+        qx(1, 1)
+        mm1(0, 0)
+        mm1(0, 1)
+        tw1(3, 0, scopy)
+        tw1(3, 1, vcopy)
+        qw1(2)
         qh(0, 0)
+        mm1(0, 2)
+        mm1(0, 3)
+        qw1(3)
+        for q in range(4):
+            tw2q(0, q, vcopy if q % 2 else scopy)
         qh(0, 1)
-        for c in range(4):
-            mm1(1, c)
-            if c == 1:
-                qh(1, 0)
-        for i in range(2):
-            for q in range(4):
-                tw2q(i, q, vcopy if q % 2 else scopy)
-                if i == 0 and q == 1:
-                    qh(1, 1)
-            qw2(i)
+        mm1(1, 0)
+        mm1(1, 1)
+        qw2(0)
+        mm1(1, 2)
+        qh(1, 0)
+        mm1(1, 3)
+        for q in range(4):
+            tw2q(1, q, vcopy if q % 2 else scopy)
+            if q == 1:
+                qh(1, 1)
+        qw2(1)
 
         back = {3: (0, 0), 4: (0, 1), 5: (1, 0), 6: (1, 1)}
-        late = ["kk", "kk", "kk", "tp", "tp", "tp", "tp", "kk"]
         for i in range(8):
             if i + 2 < 8:
                 for q in range(4):
                     tw2q(i + 2, q, scopy)
             if i in back:
-                bt(back[i][0], back[i][1], "ob")
+                bt(back[i][0], back[i][1])
             for w in range(4):
                 if w == 3 and i + 2 < 8:
                     qw2(i + 2)
-                mx(i, w, late[(i - 6) * 4 + w] if i >= 6 else "kk")
-            if i < 7:
+                mx(i, w)
+            if i < 6:
                 add(i)
-        bt(2, 0, "ob")
-        bt(2, 1, "kk")
-        ob0 = bank("kk")
-        ob1 = bank("tp")
+        bt(2, 0)
+        bt(2, 1)
+        ob0 = bank()
+        ob1 = bank()
         bt_part(ob0, 3, 0, 0)
         bt_part(ob1, 3, 1, 0)
         bt_part(ob0, 3, 0, 1)

@@ -51,6 +51,8 @@ def tile_dynamicshortconvolution_kernel(tc, x, w1, w2_w, w2_b, out):
             out=bias_bf[:].rearrange("p (u j) -> p u j", u=4),
             in_=w2_b.rearrange("(u p j) -> p u j", u=4, p=P, j=8),
         )
+        zeros = const.tile([P, 640], BF16, name="zeros")
+        nc.vector.memset(zeros[:], 0.0)
         warm = const.tile([P, 2], F32, name="warm")
         nc.vector.memset(warm[:], 0.0)
         nc.scalar.activation(out=warm[:, 1:2], in_=warm[:, 0:1], func=ACT.Silu)
@@ -264,20 +266,31 @@ def tile_dynamicshortconvolution_kernel(tc, x, w1, w2_w, w2_b, out):
             bt_part(ob, u, cp, 1)
             bt_fin(ob, u, cp)
 
+        def idle_work(n):
+            db = bank()
+            for k in range(n):
+                nc.tensor.matmul(out=db[:], lhsT=zeros[:, 0:128], rhs=zeros[:, 128:640], start=True, stop=True)
+
+        idle_work(6)
         tw1(0, 0, scopy)
         tw1(0, 1, vcopy)
+        idle_work(1)
         tw1(1, 0, scopy)
         tw1(1, 1, vcopy)
         qw1(0)
+        idle_work(1)
         tx(0, scopy)
         tx(1, scopy)
         qw1(1)
+        idle_work(1)
         tx(2, scopy)
         qx(0, 0)
         qx(1, 0)
         tx(3, scopy)
+        idle_work(1)
         tw1(2, 0, scopy)
         tw1(2, 1, vcopy)
+        idle_work(1)
         qx(0, 1)
         qx(1, 1)
         mm1(0, 0)

@@ -46,11 +46,6 @@ def tile_dynamicshortconvolution_kernel(tc, x, w1, w2_w, w2_b, out):
             taken.append(k)
             return psum.tile([P, 512], F32, name="bank%d" % k, tag="bank%d" % k)
 
-        bias_bf = const.tile([P, 32], BF16, name="bias_bf")
-        nc.scalar.dma_start(
-            out=bias_bf[:].rearrange("p (u j) -> p u j", u=4),
-            in_=w2_b.rearrange("(u p j) -> p u j", u=4, p=P, j=8),
-        )
         zeros = const.tile([P, 640], BF16, name="zeros")
         nc.vector.memset(zeros[:], 0.0)
         warm = const.tile([P, 2], F32, name="warm")
@@ -86,6 +81,11 @@ def tile_dynamicshortconvolution_kernel(tc, x, w1, w2_w, w2_b, out):
             load_x(c)
         load_w1(2)
         load_w1(3)
+        bias_bf = const.tile([P, 32], BF16, name="bias_bf")
+        nc.sync.dma_start(
+            out=bias_bf[:].rearrange("p (u j) -> p u j", u=4),
+            in_=w2_b.rearrange("(u p j) -> p u j", u=4, p=P, j=8),
+        )
         w2_sb = []
         for i in range(8):
             u, e = divmod(i, 2)
@@ -97,7 +97,6 @@ def tile_dynamicshortconvolution_kernel(tc, x, w1, w2_w, w2_b, out):
             w2_sb.append(t[:].bitcast(F32))
 
         bias = const.tile([P, 32], F32, name="bias")
-        nc.vector.tensor_copy(out=bias[:], in_=bias_bf[:])
 
         xc = keep.tile([P, 2 * TOK], U32, name="xc", align_bytes=64)
         xs = keep.tile([P, 2 * TOK], U8, name="xs", align_bytes=64)
@@ -260,6 +259,26 @@ def tile_dynamicshortconvolution_kernel(tc, x, w1, w2_w, w2_b, out):
                 in_=ot[:].rearrange("p (c d) -> p c d", c=2),
             )
 
+        def last_part(ob, c, e):
+            for k in range(4):
+                nc.tensor.matmul(
+                    out=ob[:, e * 128 : e * 128 + 128],
+                    lhsT=prod[6 + e][:, k * 512 + 128 * c : k * 512 + 128 * c + 128],
+                    rhs=ident[:],
+                    is_transpose=True,
+                    start=(k == 0),
+                    stop=(k == 3),
+                )
+
+        def last_fin(ob, c):
+            ot = outp.tile([P, 256], F32, name="ol", tag="ol")
+            nc.scalar.activation(
+                out=ot[:].rearrange("t (p e) -> t p e", e=2),
+                in_=ob[:, 0:256].rearrange("t (e p) -> t p e", e=2),
+                func=ACT.Silu,
+            )
+            nc.sync.dma_start(out=of[128 * c : 128 * c + 128, 768:1024], in_=ot[:])
+
         def bt(u, cp):
             ob = bank()
             bt_part(ob, u, cp, 0)
@@ -302,6 +321,7 @@ def tile_dynamicshortconvolution_kernel(tc, x, w1, w2_w, w2_b, out):
         mm1(0, 2)
         mm1(0, 3)
         qw1(3)
+        nc.vector.tensor_copy(out=bias[:], in_=bias_bf[:])
         for q in range(4):
             tw2q(0, q, vcopy if q % 2 else scopy)
         qh(0, 1)
@@ -332,11 +352,9 @@ def tile_dynamicshortconvolution_kernel(tc, x, w1, w2_w, w2_b, out):
                 add(i)
         bt(2, 0)
         bt(2, 1)
-        ob0 = bank()
-        ob1 = bank()
-        bt_part(ob0, 3, 0, 0)
-        bt_part(ob1, 3, 1, 0)
-        bt_part(ob0, 3, 0, 1)
-        bt_fin(ob0, 3, 0)
-        bt_part(ob1, 3, 1, 1)
-        bt_fin(ob1, 3, 1)
+        last = [bank() for c in range(4)]
+        for c in range(4):
+            last_part(last[c], c, 0)
+        for c in range(4):
+            last_part(last[c], c, 1)
+            last_fin(last[c], c)

from contextlib import ExitStack

import concourse.mybir as mybir
from concourse.masks import make_identity

F32 = mybir.dt.float32
BF16 = mybir.dt.bfloat16
U32 = mybir.dt.uint32
U8 = mybir.dt.uint8
FP8X4 = mybir.dt.float8_e4m3fn_x4
ACT = mybir.ActivationFunctionType
ALU = mybir.AluOpType

P = 128
TOK = 512
D = 1024
H = 1024
W = 4
PAD = 8
TB = 256 + PAD

FLOPS = 2 * TOK * D * H + 2 * TOK * H * D * W


def tile_dynamicshortconvolution_kernel(tc, x, w1, w2_w, w2_b, out):
    nc = tc.nc
    xf = x.flatten_outer_dims()
    of = out.flatten_outer_dims()

    with ExitStack() as ctx:
        const = ctx.enter_context(tc.tile_pool(name="const", bufs=1))
        raw = ctx.enter_context(tc.tile_pool(name="raw", bufs=1))
        keep = ctx.enter_context(tc.tile_pool(name="keep", bufs=1))
        w1gp = ctx.enter_context(tc.tile_pool(name="w1gp", bufs=3))
        w2gp = ctx.enter_context(tc.tile_pool(name="w2gp", bufs=2))
        w2cp = ctx.enter_context(tc.tile_pool(name="w2cp", bufs=4))
        prodp = ctx.enter_context(tc.tile_pool(name="prodp", bufs=3))
        sump = ctx.enter_context(tc.tile_pool(name="sump", bufs=4))
        outp = ctx.enter_context(tc.tile_pool(name="outp", bufs=4))
        psum = ctx.enter_context(tc.psum_pool(name="psum", bufs=1))
        ctx.enter_context(tc.manual_schedule())
        taken = []

        def bank():
            k = len(taken) % 8
            taken.append(k)
            return psum.tile([P, 512], F32, name="bank%d" % k, tag="bank%d" % k)

        zeros = const.tile([P, 640], BF16, name="zeros")
        nc.vector.memset(zeros[:], 0.0)
        warm = const.tile([P, 2], F32, name="warm")
        nc.vector.memset(warm[:], 0.0)
        nc.scalar.activation(out=warm[:, 1:2], in_=warm[:, 0:1], func=ACT.Silu)
        ident = const.tile([P, P], F32, name="ident")
        make_identity(nc, ident[:])

        xg = keep.tile([P, 4 * TB * 4], BF16, name="xg", align_bytes=64)
        xgw = xg[:].bitcast(F32).rearrange("p (g b t u) -> p g b t u", g=2, b=2, t=TB, u=2)
        xgq = xg[:].rearrange("p (g b t q) -> p g b t q", g=2, b=2, t=TB, q=4)
        nc.gpsimd.memset(xgw[:, :, :, 0:PAD, :], 0.0)

        x_sb = []
        w1_sb = []

        def load_x(c):
            t = raw.tile([P, D], BF16, name="x_sb%d" % c)
            nc.sync.dma_start(out=t[:], in_=xf[128 * c : 128 * c + 128, :])
            x_sb.append(t[:].bitcast(F32))

        def load_w1(a):
            t = raw.tile([P, 2 * D], BF16, name="w1_sb%d" % a)
            nc.sync.dma_start(
                out=t[:].rearrange("p (e d) -> p e d", e=2),
                in_=w1[256 * a : 256 * a + 256, :].rearrange("(p e) d -> p e d", e=2),
            )
            w1_sb.append(t[:].bitcast(F32))

        load_w1(0)
        load_w1(1)
        for c in range(4):
            load_x(c)
        load_w1(2)
        load_w1(3)
        bias_bf = const.tile([P, 32], BF16, name="bias_bf")
        nc.sync.dma_start(
            out=bias_bf[:].rearrange("p (u j) -> p u j", u=4),
            in_=w2_b.rearrange("(u p j) -> p u j", u=4, p=P, j=8),
        )
        w2_sb = []
        for i in range(8):
            u, e = divmod(i, 2)
            t = raw.tile([P, 4 * H], BF16, name="w2_sb%d" % i)
            nc.sync.dma_start(
                out=t[:].rearrange("p (j h) -> p j h", j=4),
                in_=w2_w[1024 * u : 1024 * u + 1024, :].rearrange("(p j) h -> p j h", j=8)[:, 4 * e : 4 * e + 4, :],
            )
            w2_sb.append(t[:].bitcast(F32))

        bias = const.tile([P, 32], F32, name="bias")

        xc = keep.tile([P, 2 * TOK], U32, name="xc", align_bytes=64)
        xs = keep.tile([P, 2 * TOK], U8, name="xs", align_bytes=64)
        w1c = keep.tile([P, 4 * 512], U32, name="w1c", align_bytes=64)
        w1s = keep.tile([P, 4 * 512], U8, name="w1s", align_bytes=64)
        hg = [keep.tile([P, TOK * 4], BF16, name="hg%d" % g, align_bytes=64) for g in range(2)]
        hc = keep.tile([P, 2 * TOK], U32, name="hc", align_bytes=64)
        hs = keep.tile([P, 2 * TOK], U8, name="hs", align_bytes=64)

        vcopy = nc.vector.tensor_copy
        scopy = nc.scalar.copy

        def transposes(src, offsets):
            tp = bank()
            for k, off in enumerate(offsets):
                nc.tensor.transpose(tp[:, 128 * k : 128 * k + 128], src[:, off : off + 128], ident[:])
            return tp

        def regroup(eng_copy, dst_words, tp):
            eng_copy(
                out=dst_words.rearrange("p (c u) -> p c u", u=2),
                in_=tp[:].rearrange("p (u c) -> p c u", u=2),
            )

        def quant(src, codes, scales, lo, n):
            nc.vector.quantize_mx(
                out=codes[:, lo : lo + n].bitcast(FP8X4), scales=scales[:, lo : lo + n], in_=src
            )

        def tx(c, eng_copy):
            tp = transposes(x_sb[c], [256 * g + 128 * u for g in range(2) for u in range(2)])
            b, cc = divmod(c, 2)
            lo = PAD + 128 * cc
            eng_copy(
                out=xgw[:, :, b, lo : lo + 128, :],
                in_=tp[:].rearrange("p (g u t) -> p g t u", g=2, u=2),
            )

        def qx(g, b):
            lo = ((g * 2 + b) * TB + PAD) * 4
            quant(xg[:, lo : lo + 1024], xc, xs, g * 512 + 256 * b, 256)

        w1g = {}

        def tw1(a, g, eng_copy):
            if g == 0:
                w1g[a] = w1gp.tile([P, 2048], BF16, name="w1g", tag="w1g", align_bytes=64)
            gw = w1g[a][:].bitcast(F32)
            tp = transposes(w1_sb[a], [e * 512 + 256 * g + 128 * u for u in range(2) for e in range(2)])
            regroup(eng_copy, gw[:, g * 512 : g * 512 + 512], tp)

        def qw1(a):
            quant(w1g[a][:], w1c, w1s, a * 512, 512)

        w2g = {}
        w2c = {}
        w2s = {}

        def tw2q(i, q, eng_copy):
            if q == 0:
                w2g[i] = w2gp.tile([P, 4096], BF16, name="w2g", tag="w2g", align_bytes=64)
            gw = w2g[i][:].bitcast(F32)
            gg, wp = divmod(q, 2)
            tp = transposes(
                w2_sb[i], [(2 * wp + ww) * 512 + 256 * gg + 128 * u for u in range(2) for ww in range(2)]
            )
            regroup(eng_copy, gw[:, q * 512 : q * 512 + 512], tp)

        def qw2(i):
            w2c[i] = w2cp.tile([P, 1024], U32, name="w2c", tag="w2c", align_bytes=64)
            w2s[i] = w2cp.tile([P, 1024], U8, name="w2s", tag="w2s", align_bytes=64)
            quant(w2g[i][:], w2c[i], w2s[i], 0, 1024)

        def mm1(gg, c):
            kk = bank()
            for t in range(4):
                a = 2 * gg + t // 2
                e = t % 2
                for g in range(2):
                    lo = a * 512 + g * 256 + e * 128
                    ro = g * 512 + 128 * c
                    nc.tensor.matmul_mx(
                        out=kk[:, 128 * t : 128 * t + 128],
                        lhsT=w1c[:, lo : lo + 128].bitcast(FP8X4),
                        lhsT_scale=w1s[:, lo : lo + 128],
                        rhs=xc[:, ro : ro + 128].bitcast(FP8X4),
                        rhs_scale=xs[:, ro : ro + 128],
                        start=(g == 0),
                        stop=(g == 1),
                    )
            nc.scalar.activation(
                out=hg[gg][:, c * 512 : c * 512 + 512].rearrange("p (r t) -> p r t", t=4),
                in_=kk[:].rearrange("p (t r) -> p r t", t=4),
                func=ACT.Silu,
            )

        def qh(gg, half):
            quant(hg[gg][:, half * 1024 : half * 1024 + 1024], hc, hs, gg * 512 + half * 256, 256)

        prod = {}
        sums = {}

        def mx(i, w):
            u, e = divmod(i, 2)
            if w == 0:
                prod[i] = prodp.tile([P, 4 * TOK], F32, name="prod", tag="prod")
            kk = bank()
            for gg in range(2):
                lo = gg * 512 + w * 128
                nc.tensor.matmul_mx(
                    out=kk[:],
                    lhsT=w2c[i][:, lo : lo + 128].bitcast(FP8X4),
                    lhsT_scale=w2s[i][:, lo : lo + 128],
                    rhs=hc[:, gg * 512 : gg * 512 + 512].bitcast(FP8X4),
                    rhs_scale=hs[:, gg * 512 : gg * 512 + 512],
                    start=(gg == 0),
                    stop=(gg == 1),
                )
            col = u * 8 + 4 * e + w
            nc.vector.scalar_tensor_tensor(
                out=prod[i][:, w * 512 : w * 512 + 512].rearrange("p (b t) -> p b t", b=2),
                in0=kk[:].rearrange("p (b t) -> p b t", b=2),
                scalar=bias[:, col : col + 1],
                in1=xgq[:, u // 2, :, PAD - 3 + w : PAD - 3 + w + 256, 2 * (u % 2) + e],
                op0=ALU.add,
                op1=ALU.mult,
            )

        def add(i):
            sums[i] = sump.tile([P, 2 * TOK], F32, name="sums", tag="sums")
            nc.gpsimd.tensor_tensor(
                out=sums[i][:], in0=prod[i][:, 0:1024], in1=prod[i][:, 1024:2048], op=ALU.add
            )

        def bt_part(ob, u, cp, e):
            i = 2 * u + e
            src, n = (sums[i], 2) if i in sums else (prod[i], 4)
            for cc in range(2):
                c = 2 * cp + cc
                lo = cc * 256 + e * 128
                for k in range(n):
                    nc.tensor.matmul(
                        out=ob[:, lo : lo + 128],
                        lhsT=src[:, k * 512 + 128 * c : k * 512 + 128 * c + 128],
                        rhs=ident[:],
                        is_transpose=True,
                        start=(k == 0),
                        stop=(k == n - 1),
                    )

        def bt_fin(ob, u, cp):
            ot = outp.tile([P, 512], F32, name="ot", tag="ot")
            nc.scalar.activation(
                out=ot[:].rearrange("t (c p e) -> t c p e", c=2, e=2),
                in_=ob[:].rearrange("t (c e p) -> t c p e", c=2, e=2),
                func=ACT.Silu,
            )
            nc.sync.dma_start(
                out=of[256 * cp : 256 * cp + 256, 256 * u : 256 * u + 256].rearrange("(c p) d -> p c d", p=P),
                in_=ot[:].rearrange("p (c d) -> p c d", c=2),
            )

        def last_part(ob, c, e):
            for k in range(4):
                nc.tensor.matmul(
                    out=ob[:, e * 128 : e * 128 + 128],
                    lhsT=prod[6 + e][:, k * 512 + 128 * c : k * 512 + 128 * c + 128],
                    rhs=ident[:],
                    is_transpose=True,
                    start=(k == 0),
                    stop=(k == 3),
                )

        def last_fin(ob, c):
            ot = outp.tile([P, 256], F32, name="ol", tag="ol")
            nc.scalar.activation(
                out=ot[:].rearrange("t (p e) -> t p e", e=2),
                in_=ob[:, 0:256].rearrange("t (e p) -> t p e", e=2),
                func=ACT.Silu,
            )
            nc.sync.dma_start(out=of[128 * c : 128 * c + 128, 768:1024], in_=ot[:])

        def bt(u, cp):
            ob = bank()
            bt_part(ob, u, cp, 0)
            bt_part(ob, u, cp, 1)
            bt_fin(ob, u, cp)

        def idle_work(n):
            db = bank()
            for k in range(n):
                nc.tensor.matmul(out=db[:], lhsT=zeros[:, 0:128], rhs=zeros[:, 128:640], start=True, stop=True)

        idle_work(6)
        tw1(0, 0, scopy)
        tw1(0, 1, vcopy)
        idle_work(1)
        tw1(1, 0, scopy)
        tw1(1, 1, vcopy)
        qw1(0)
        idle_work(1)
        tx(0, scopy)
        tx(1, scopy)
        qw1(1)
        idle_work(1)
        tx(2, scopy)
        qx(0, 0)
        qx(1, 0)
        tx(3, scopy)
        idle_work(1)
        tw1(2, 0, scopy)
        tw1(2, 1, vcopy)
        idle_work(1)
        qx(0, 1)
        qx(1, 1)
        mm1(0, 0)
        mm1(0, 1)
        tw1(3, 0, scopy)
        tw1(3, 1, vcopy)
        qw1(2)
        qh(0, 0)
        mm1(0, 2)
        mm1(0, 3)
        qw1(3)
        nc.vector.tensor_copy(out=bias[:], in_=bias_bf[:])
        for q in range(4):
            tw2q(0, q, vcopy if q % 2 else scopy)
        qh(0, 1)
        mm1(1, 0)
        mm1(1, 1)
        qw2(0)
        mm1(1, 2)
        qh(1, 0)
        mm1(1, 3)
        for q in range(4):
            tw2q(1, q, vcopy if q % 2 else scopy)
            if q == 1:
                qh(1, 1)
        qw2(1)

        back = {3: (0, 0), 4: (0, 1), 5: (1, 0), 6: (1, 1)}
        for i in range(8):
            if i + 2 < 8:
                for q in range(4):
                    tw2q(i + 2, q, scopy)
            if i in back:
                bt(back[i][0], back[i][1])
            for w in range(4):
                if w == 3 and i + 2 < 8:
                    qw2(i + 2)
                mx(i, w)
            if i < 6:
                add(i)
        bt(2, 0)
        bt(2, 1)
        last = [bank() for c in range(4)]
        for c in range(4):
            last_part(last[c], c, 0)
        for c in range(4):
            last_part(last[c], c, 1)
            last_fin(last[c], c)
